import numpy as np
import ml_dtypes


def mxq(x, axis, fmt="e4m3"):
    dtype, down = {"e4m3": (ml_dtypes.float8_e4m3fn, 7), "e5m2": (ml_dtypes.float8_e5m2, 14)}[fmt]
    v = np.moveaxis(np.asarray(x, np.float32).astype(ml_dtypes.bfloat16).astype(np.float64), axis, -1)
    blocks = v.reshape(v.shape[:-1] + (-1, 32))
    amax = np.abs(blocks).max(-1, keepdims=True)
    byte = np.maximum(np.where(amax > 0, np.frexp(amax)[1] - 1 + 127, 0) - down, 1)
    scale = np.exp2(byte - 127.0)
    codes = (blocks / scale).astype(np.float32).astype(dtype).astype(np.float64)
    return np.moveaxis((codes * scale).reshape(v.shape), -1, axis)


WIDE = False


def mx_kscale(k):
    if not WIDE:
        return np.ones(k)
    levels = np.array([10, -10, 5, -5, 0])
    a = np.random.permutation(np.resize(levels, k // 512 * 4)).reshape(k // 512, 4)
    idx = np.arange(k)
    return np.exp2(a[idx // 512, idx % 128 // 32])


BF16 = ml_dtypes.bfloat16


def bf(x):
    return np.asarray(x, np.float32).astype(BF16)


def f64(x):
    return np.asarray(x).astype(np.float64)


B, STACK, TUBE, CH, IMG, PATCH, EMBED = 4, 16, 2, 1, 256, 64, 512
GH = IMG // PATCH
GW = IMG // PATCH
GD = STACK // TUBE
K = TUBE * CH * PATCH * PATCH


def _sincos_1d(dim, pos):
    omega = 1.0 / (10000.0 ** (np.arange(dim // 2, dtype=np.float64) / (dim / 2.0)))
    out = pos[:, None].astype(np.float64) * omega[None, :]
    return np.concatenate([np.sin(out), np.cos(out)], axis=1)


def get_3d_sincos_pos_embed(grid_h, grid_w, grid_depth, embed_dim):
    dim_t = embed_dim // 4
    dim_s = embed_dim - dim_t
    emb_t = _sincos_1d(dim_t, np.arange(grid_depth))
    emb_h = _sincos_1d(dim_s // 2, np.arange(grid_h))
    emb_w = _sincos_1d(dim_s - dim_s // 2, np.arange(grid_w))
    emb_hw = np.concatenate([np.repeat(emb_h, grid_w, axis=0), np.tile(emb_w, (grid_h, 1))], axis=1)
    ns = grid_h * grid_w
    return np.concatenate([np.repeat(emb_t, ns, axis=0), np.tile(emb_hw, (grid_depth, 1))], axis=1)


def setup_inputs():
    s = mx_kscale(K)
    sv = s.reshape(TUBE, CH, PATCH, PATCH)[:, :, None, :, None, :]
    video = np.random.standard_normal((B, GD, TUBE, CH, GH, PATCH, GW, PATCH)) * sv
    return {"video": bf(video.reshape(B, STACK, CH, IMG, IMG)),
            "W": bf(np.random.standard_normal((EMBED, K)) / np.sqrt(K) / s[None, :]),
            "b": bf(np.random.standard_normal(EMBED) * 0.3),
            "pos_embed": bf(get_3d_sincos_pos_embed(GH, GW, GD, EMBED)[None])}


def reference(video, W, b, pos_embed):
    video = f64(video)
    B_, T, C, H, W_ = video.shape
    p = PATCH
    gh, gw = H // p, W_ // p
    ns = gh * gw
    x = video.reshape(B_ * T, C, gh, p, gw, p)
    x = x.transpose(0, 2, 4, 1, 3, 5)
    x = x.reshape(B_, T, ns, C * p * p)
    x = x.reshape(B_, GD, TUBE, ns, C * p * p)
    x = x.transpose(0, 1, 3, 2, 4)
    tubelets = x.reshape(B_, GD * ns, TUBE * C * p * p)
    tokens = (mxq(tubelets, 2, "e4m3") @ mxq(f64(W), 1, "e4m3").T) + f64(b) + f64(pos_embed)
    return tokens

@@ -1,0 +1,167 @@
+from contextlib import ExitStack
+
+import concourse.mybir as mybir
+from concourse.masks import make_identity
+
+BF16 = mybir.dt.bfloat16
+F32 = mybir.dt.float32
+U32 = mybir.dt.uint32
+U8 = mybir.dt.uint8
+FP8X4 = mybir.dt.float8_e4m3fn_x4
+
+P = 128
+BATCH, STACK, TUBE, IMG, PATCH, EMBED = 4, 16, 2, 256, 64, 512
+GRID = IMG // PATCH
+TUBES = STACK // TUBE
+K = TUBE * PATCH * PATCH
+K_PASS = 4 * P
+PASSES = K // K_PASS
+PASSES_PER_FRAME = PASSES // TUBE
+ROWS_PER_PASS = K_PASS // PATCH
+COL_TILES = 4
+COLUMNS = 2 * EMBED
+
+MULTIPLY_LAG = 2
+POS_AFTER_PASS = 8
+
+FLOPS = 2 * BATCH * TUBES * GRID * GRID * EMBED * K
+
+
+def tile_tubeletembedding_k_kernel(tc, video, W, b, pos_embed, out):
+    nc = tc.nc
+    assert tuple(video.shape) == (BATCH, STACK, 1, IMG, IMG)
+    assert tuple(W.shape) == (EMBED, K)
+    assert BATCH * TUBES * GRID == P
+
+    video_rows = video.rearrange("b (d t) c (i y) x -> t i (b d) (c y x)", t=TUBE, i=GRID)
+    w_rows = W.rearrange("(c p) k -> p c k", p=P)
+    pos_rows = pos_embed.rearrange("o (q j) e -> (o q) (j e)", j=GRID)
+    out_rows = out.rearrange("b (q j) e -> (b q) j e", j=GRID)
+
+    with ExitStack() as ctx:
+        consts = ctx.enter_context(tc.tile_pool(name="consts", bufs=1))
+        loaded = ctx.enter_context(tc.tile_pool(name="loaded", bufs=1))
+        work = ctx.enter_context(tc.tile_pool(name="work", bufs=3))
+        sums = ctx.enter_context(tc.psum_pool(name="sums", bufs=1))
+        banks = ctx.enter_context(tc.psum_pool(name="banks", bufs=4))
+        ctx.enter_context(tc.manual_schedule())
+
+        video_raw = []
+        w_raw = []
+        pos_sb = consts.tile([P, GRID * EMBED], BF16)
+        for g in range(PASSES):
+            ts, y8 = divmod(g, PASSES_PER_FRAME)
+            run = slice(y8 * ROWS_PER_PASS * IMG, (y8 + 1) * ROWS_PER_PASS * IMG)
+            v_in = loaded.tile([P, ROWS_PER_PASS * IMG], BF16, name="v_in%d" % g)
+            for i in range(GRID):
+                nc.sync.dma_start(out=v_in[i:P:GRID, :], in_=video_rows[ts, i, :, run])
+            w_in = loaded.tile([P, COL_TILES * K_PASS], BF16, name="w_in%d" % g)
+            nc.sync.dma_start(
+                out=w_in[:].rearrange("p (c k) -> p c k", c=COL_TILES),
+                in_=w_rows[:, :, g * K_PASS : (g + 1) * K_PASS],
+            )
+            video_raw.append(v_in)
+            w_raw.append(w_in)
+            if g == POS_AFTER_PASS:
+                for batch in range(BATCH):
+                    rows = slice(batch * TUBES * GRID, (batch + 1) * TUBES * GRID)
+                    nc.sync.dma_start(out=pos_sb[rows, :], in_=pos_rows)
+
+        ident = consts.tile([P, P], F32)
+        make_identity(nc, ident[:])
+
+        bias_row = consts.tile([P, EMBED], BF16)
+        nc.vector.memset(bias_row[:], 0.0)
+        nc.scalar.dma_start(out=bias_row[0:1, :], in_=b.rearrange("(o e) -> o e", o=1))
+        ones = consts.tile([P, P], BF16)
+        nc.vector.memset(ones[:], 1.0)
+        bias_bank = banks.tile([P, EMBED], F32, name="bank")
+        nc.tensor.matmul(out=bias_bank[:], lhsT=ones[:], rhs=bias_row[:], start=True, stop=True)
+        bias_all = consts.tile([P, EMBED], F32)
+        nc.scalar.copy(out=bias_all[:], in_=bias_bank[:])
+
+        addend = consts.tile([P, GRID * EMBED], F32)
+        result = consts.tile([P, GRID * EMBED], F32)
+        acc = []
+        for j in range(GRID):
+            acc_j = sums.tile([P, EMBED], F32, name="acc%d" % j)
+            acc.append(acc_j)
+
+        video_tok = {}
+        grouped = {}
+        codes = {}
+        scales = {}
+
+        def regroup(g):
+            v_tok = work.tile([P, COL_TILES * K_PASS], BF16, name="v_tok")
+            nc.vector.tensor_copy(
+                out=v_tok[:].rearrange("p (j y x) -> p j y x", j=GRID, x=PATCH),
+                in_=video_raw[g][:].rearrange("p (y j x) -> p j y x", j=GRID, x=PATCH),
+            )
+            video_tok[g] = v_tok
+
+        def transpose_and_group(source, target_words):
+            words = source[:].bitcast(F32)
+            for pair in range(COL_TILES // 2):
+                bank = banks.tile([P, 2, 2 * P], F32, name="bank")
+                for c in range(2):
+                    for u in range(2):
+                        first = ((2 * pair + c) * 2 + u) * P
+                        nc.tensor.transpose(
+                            bank[:, u, c * P : (c + 1) * P], words[:, first : first + P], ident[:]
+                        )
+                nc.scalar.copy(
+                    out=target_words[:, pair * 2 * P : (pair + 1) * 2 * P, :],
+                    in_=bank[:].rearrange("p u c -> p c u"),
+                )
+
+        def transpose(g):
+            grp = work.tile([P, COLUMNS * 4], BF16, name="grp", align_bytes=64)
+            grp_words = grp[:].bitcast(F32).rearrange("p (c u) -> p c u", u=2)
+            transpose_and_group(video_tok[g], grp_words[:, EMBED:COLUMNS, :])
+            transpose_and_group(w_raw[g], grp_words[:, 0:EMBED, :])
+            grouped[g] = grp
+
+        def quantise(g):
+            cod = work.tile([P, COLUMNS], U32, name="cod", align_bytes=64)
+            sca = work.tile([P, COLUMNS], U8, name="sca", align_bytes=64)
+            nc.vector.quantize_mx(out=cod[:].bitcast(FP8X4), scales=sca[:], in_=grouped[g][:])
+            codes[g] = cod
+            scales[g] = sca
+
+        def multiply(g):
+            for j in range(GRID):
+                tokens = slice(EMBED + j * P, EMBED + (j + 1) * P)
+                nc.tensor.matmul_mx(
+                    out=acc[j][:],
+                    lhsT=codes[g][:, tokens].bitcast(FP8X4),
+                    lhsT_scale=scales[g][:, tokens],
+                    rhs=codes[g][:, 0:EMBED].bitcast(FP8X4),
+                    rhs_scale=scales[g][:, 0:EMBED],
+                    start=(g == 0),
+                    stop=(g == PASSES - 1),
+                )
+
+        regroup(0)
+        for s in range(PASSES + MULTIPLY_LAG):
+            if s < PASSES:
+                transpose(s)
+            if 1 <= s <= PASSES:
+                quantise(s - 1)
+            if s >= MULTIPLY_LAG:
+                multiply(s - MULTIPLY_LAG)
+            if s + 1 < PASSES:
+                regroup(s + 1)
+            j = s - (POS_AFTER_PASS + 2)
+            if 0 <= j < GRID:
+                part = slice(j * EMBED, (j + 1) * EMBED)
+                nc.vector.tensor_tensor(
+                    out=addend[:, part], in0=pos_sb[:, part], in1=bias_all[:], op=mybir.AluOpType.add
+                )
+
+        for j in range(GRID):
+            part = slice(j * EMBED, (j + 1) * EMBED)
+            nc.vector.tensor_tensor(
+                out=result[:, part], in0=acc[j][:], in1=addend[:, part], op=mybir.AluOpType.add
+            )
+            nc.sync.dma_start(out=out_rows[:, j, :], in_=result[:, part])

@@ -21,7 +21,8 @@ ROWS_PER_PASS = K_PASS // PATCH
 COL_TILES = 4
 COLUMNS = 2 * EMBED
 
-MULTIPLY_LAG = 2
+LOAD_PASSES = 2
+RUN = 2
 POS_AFTER_PASS = 8
 
 FLOPS = 2 * BATCH * TUBES * GRID * GRID * EMBED * K
@@ -41,27 +42,30 @@ def tile_tubeletembedding_k_kernel(tc, video, W, b, pos_embed, out):
     with ExitStack() as ctx:
         consts = ctx.enter_context(tc.tile_pool(name="consts", bufs=1))
         loaded = ctx.enter_context(tc.tile_pool(name="loaded", bufs=1))
-        work = ctx.enter_context(tc.tile_pool(name="work", bufs=3))
+        work = ctx.enter_context(tc.tile_pool(name="work", bufs=4))
         sums = ctx.enter_context(tc.psum_pool(name="sums", bufs=1))
         banks = ctx.enter_context(tc.psum_pool(name="banks", bufs=4))
         ctx.enter_context(tc.manual_schedule())
 
+        assert PASSES_PER_FRAME % LOAD_PASSES == 0
         video_raw = []
-        w_raw = []
+        w_words = []
         pos_sb = consts.tile([P, GRID * EMBED], BF16)
-        for g in range(PASSES):
+        for g in range(0, PASSES, LOAD_PASSES):
             ts, y8 = divmod(g, PASSES_PER_FRAME)
-            run = slice(y8 * ROWS_PER_PASS * IMG, (y8 + 1) * ROWS_PER_PASS * IMG)
-            v_in = loaded.tile([P, ROWS_PER_PASS * IMG], BF16, name="v_in%d" % g)
+            run = slice(y8 * ROWS_PER_PASS * IMG, (y8 + LOAD_PASSES) * ROWS_PER_PASS * IMG)
+            v_in = loaded.tile([P, LOAD_PASSES * ROWS_PER_PASS * IMG], BF16, name="v_in%d" % g)
             for i in range(GRID):
                 nc.sync.dma_start(out=v_in[i:P:GRID, :], in_=video_rows[ts, i, :, run])
-            w_in = loaded.tile([P, COL_TILES * K_PASS], BF16, name="w_in%d" % g)
+            w_in = loaded.tile([P, COL_TILES * LOAD_PASSES * K_PASS], BF16, name="w_in%d" % g)
             nc.sync.dma_start(
                 out=w_in[:].rearrange("p (c k) -> p c k", c=COL_TILES),
-                in_=w_rows[:, :, g * K_PASS : (g + 1) * K_PASS],
+                in_=w_rows[:, :, g * K_PASS : (g + LOAD_PASSES) * K_PASS],
             )
-            video_raw.append(v_in)
-            w_raw.append(w_in)
+            w_in_words = w_in[:].bitcast(F32).rearrange("p (c k) -> p c k", c=COL_TILES)
+            for n in range(LOAD_PASSES):
+                video_raw.append(v_in[:, n * ROWS_PER_PASS * IMG : (n + 1) * ROWS_PER_PASS * IMG])
+                w_words.append(w_in_words[:, :, n * K_PASS // 2 : (n + 1) * K_PASS // 2])
             if g == POS_AFTER_PASS:
                 for batch in range(BATCH):
                     rows = slice(batch * TUBES * GRID, (batch + 1) * TUBES * GRID)
@@ -96,30 +100,33 @@ def tile_tubeletembedding_k_kernel(tc, video, W, b, pos_embed, out):
             v_tok = work.tile([P, COL_TILES * K_PASS], BF16, name="v_tok")
             nc.vector.tensor_copy(
                 out=v_tok[:].rearrange("p (j y x) -> p j y x", j=GRID, x=PATCH),
-                in_=video_raw[g][:].rearrange("p (y j x) -> p j y x", j=GRID, x=PATCH),
+                in_=video_raw[g].rearrange("p (y j x) -> p j y x", j=GRID, x=PATCH),
             )
             video_tok[g] = v_tok
 
-        def transpose_and_group(source, target_words):
-            words = source[:].bitcast(F32)
+        def transpose_and_group(words, target_words, vector_takes_last):
             for pair in range(COL_TILES // 2):
                 bank = banks.tile([P, 2, 2 * P], F32, name="bank")
                 for c in range(2):
                     for u in range(2):
-                        first = ((2 * pair + c) * 2 + u) * P
                         nc.tensor.transpose(
-                            bank[:, u, c * P : (c + 1) * P], words[:, first : first + P], ident[:]
+                            bank[:, u, c * P : (c + 1) * P],
+                            words[:, 2 * pair + c, u * P : (u + 1) * P],
+                            ident[:],
                         )
-                nc.scalar.copy(
-                    out=target_words[:, pair * 2 * P : (pair + 1) * 2 * P, :],
-                    in_=bank[:].rearrange("p u c -> p c u"),
-                )
+                columns = slice(pair * 2 * P, (pair + 1) * 2 * P)
+                planes = bank[:].rearrange("p u c -> p c u")
+                if vector_takes_last and pair == COL_TILES // 2 - 1:
+                    nc.vector.tensor_copy(out=target_words[:, columns, :], in_=planes)
+                else:
+                    nc.scalar.copy(out=target_words[:, columns, :], in_=planes)
 
         def transpose(g):
             grp = work.tile([P, COLUMNS * 4], BF16, name="grp", align_bytes=64)
             grp_words = grp[:].bitcast(F32).rearrange("p (c u) -> p c u", u=2)
-            transpose_and_group(video_tok[g], grp_words[:, EMBED:COLUMNS, :])
-            transpose_and_group(w_raw[g], grp_words[:, 0:EMBED, :])
+            tok_words = video_tok[g][:].bitcast(F32).rearrange("p (c k) -> p c k", c=COL_TILES)
+            transpose_and_group(tok_words, grp_words[:, EMBED:COLUMNS, :], False)
+            transpose_and_group(w_words[g], grp_words[:, 0:EMBED, :], g % 2 == 0)
             grouped[g] = grp
 
         def quantise(g):
@@ -129,29 +136,31 @@ def tile_tubeletembedding_k_kernel(tc, video, W, b, pos_embed, out):
             codes[g] = cod
             scales[g] = sca
 
-        def multiply(g):
+        def multiply(passes):
             for j in range(GRID):
                 tokens = slice(EMBED + j * P, EMBED + (j + 1) * P)
-                nc.tensor.matmul_mx(
-                    out=acc[j][:],
-                    lhsT=codes[g][:, tokens].bitcast(FP8X4),
-                    lhsT_scale=scales[g][:, tokens],
-                    rhs=codes[g][:, 0:EMBED].bitcast(FP8X4),
-                    rhs_scale=scales[g][:, 0:EMBED],
-                    start=(g == 0),
-                    stop=(g == PASSES - 1),
-                )
+                for g in passes:
+                    nc.tensor.matmul_mx(
+                        out=acc[j][:],
+                        lhsT=codes[g][:, tokens].bitcast(FP8X4),
+                        lhsT_scale=scales[g][:, tokens],
+                        rhs=codes[g][:, 0:EMBED].bitcast(FP8X4),
+                        rhs_scale=scales[g][:, 0:EMBED],
+                        start=(g == 0),
+                        stop=(g == PASSES - 1),
+                    )
 
         regroup(0)
-        for s in range(PASSES + MULTIPLY_LAG):
-            if s < PASSES:
-                transpose(s)
+        regroup(1)
+        for s in range(PASSES + RUN):
             if 1 <= s <= PASSES:
                 quantise(s - 1)
-            if s >= MULTIPLY_LAG:
-                multiply(s - MULTIPLY_LAG)
-            if s + 1 < PASSES:
-                regroup(s + 1)
+            if s + 2 < PASSES:
+                regroup(s + 2)
+            if s < PASSES:
+                transpose(s)
+            if s % RUN == RUN - 1 and s >= 2 * RUN - 1:
+                multiply(range(s - 2 * RUN + 1, s - RUN + 1))
             j = s - (POS_AFTER_PASS + 2)
             if 0 <= j < GRID:
                 part = slice(j * EMBED, (j + 1) * EMBED)

@@ -21,8 +21,7 @@ ROWS_PER_PASS = K_PASS // PATCH
 COL_TILES = 4
 COLUMNS = 2 * EMBED
 
-LOAD_PASSES = 2
-RUN = 2
+MULTIPLY_LAG = 2
 POS_AFTER_PASS = 8
 
 FLOPS = 2 * BATCH * TUBES * GRID * GRID * EMBED * K
@@ -42,30 +41,27 @@ def tile_tubeletembedding_k_kernel(tc, video, W, b, pos_embed, out):
     with ExitStack() as ctx:
         consts = ctx.enter_context(tc.tile_pool(name="consts", bufs=1))
         loaded = ctx.enter_context(tc.tile_pool(name="loaded", bufs=1))
-        work = ctx.enter_context(tc.tile_pool(name="work", bufs=4))
+        work = ctx.enter_context(tc.tile_pool(name="work", bufs=3))
         sums = ctx.enter_context(tc.psum_pool(name="sums", bufs=1))
         banks = ctx.enter_context(tc.psum_pool(name="banks", bufs=4))
         ctx.enter_context(tc.manual_schedule())
 
-        assert PASSES_PER_FRAME % LOAD_PASSES == 0
         video_raw = []
-        w_words = []
+        w_raw = []
         pos_sb = consts.tile([P, GRID * EMBED], BF16)
-        for g in range(0, PASSES, LOAD_PASSES):
+        for g in range(PASSES):
             ts, y8 = divmod(g, PASSES_PER_FRAME)
-            run = slice(y8 * ROWS_PER_PASS * IMG, (y8 + LOAD_PASSES) * ROWS_PER_PASS * IMG)
-            v_in = loaded.tile([P, LOAD_PASSES * ROWS_PER_PASS * IMG], BF16, name="v_in%d" % g)
+            run = slice(y8 * ROWS_PER_PASS * IMG, (y8 + 1) * ROWS_PER_PASS * IMG)
+            v_in = loaded.tile([P, ROWS_PER_PASS * IMG], BF16, name="v_in%d" % g)
             for i in range(GRID):
                 nc.sync.dma_start(out=v_in[i:P:GRID, :], in_=video_rows[ts, i, :, run])
-            w_in = loaded.tile([P, COL_TILES * LOAD_PASSES * K_PASS], BF16, name="w_in%d" % g)
+            w_in = loaded.tile([P, COL_TILES * K_PASS], BF16, name="w_in%d" % g)
             nc.sync.dma_start(
                 out=w_in[:].rearrange("p (c k) -> p c k", c=COL_TILES),
-                in_=w_rows[:, :, g * K_PASS : (g + LOAD_PASSES) * K_PASS],
+                in_=w_rows[:, :, g * K_PASS : (g + 1) * K_PASS],
             )
-            w_in_words = w_in[:].bitcast(F32).rearrange("p (c k) -> p c k", c=COL_TILES)
-            for n in range(LOAD_PASSES):
-                video_raw.append(v_in[:, n * ROWS_PER_PASS * IMG : (n + 1) * ROWS_PER_PASS * IMG])
-                w_words.append(w_in_words[:, :, n * K_PASS // 2 : (n + 1) * K_PASS // 2])
+            video_raw.append(v_in)
+            w_raw.append(w_in)
             if g == POS_AFTER_PASS:
                 for batch in range(BATCH):
                     rows = slice(batch * TUBES * GRID, (batch + 1) * TUBES * GRID)
@@ -99,34 +95,31 @@ def tile_tubeletembedding_k_kernel(tc, video, W, b, pos_embed, out):
         def regroup(g):
             v_tok = work.tile([P, COL_TILES * K_PASS], BF16, name="v_tok")
             nc.vector.tensor_copy(
-                out=v_tok[:].rearrange("p (j y x) -> p j y x", j=GRID, x=PATCH),
-                in_=video_raw[g].rearrange("p (y j x) -> p j y x", j=GRID, x=PATCH),
+                out=v_tok[:].bitcast(F32).rearrange("p (j y w) -> p j y w", j=GRID, w=PATCH // 2),
+                in_=video_raw[g][:].bitcast(F32).rearrange("p (y j w) -> p j y w", j=GRID, w=PATCH // 2),
             )
             video_tok[g] = v_tok
 
-        def transpose_and_group(words, target_words, vector_takes_last):
+        def transpose_and_group(source, target_words):
+            words = source[:].bitcast(F32)
             for pair in range(COL_TILES // 2):
                 bank = banks.tile([P, 2, 2 * P], F32, name="bank")
                 for c in range(2):
                     for u in range(2):
+                        first = ((2 * pair + c) * 2 + u) * P
                         nc.tensor.transpose(
-                            bank[:, u, c * P : (c + 1) * P],
-                            words[:, 2 * pair + c, u * P : (u + 1) * P],
-                            ident[:],
+                            bank[:, u, c * P : (c + 1) * P], words[:, first : first + P], ident[:]
                         )
-                columns = slice(pair * 2 * P, (pair + 1) * 2 * P)
-                planes = bank[:].rearrange("p u c -> p c u")
-                if vector_takes_last and pair == COL_TILES // 2 - 1:
-                    nc.vector.tensor_copy(out=target_words[:, columns, :], in_=planes)
-                else:
-                    nc.scalar.copy(out=target_words[:, columns, :], in_=planes)
+                nc.scalar.copy(
+                    out=target_words[:, pair * 2 * P : (pair + 1) * 2 * P, :],
+                    in_=bank[:].rearrange("p u c -> p c u"),
+                )
 
         def transpose(g):
             grp = work.tile([P, COLUMNS * 4], BF16, name="grp", align_bytes=64)
             grp_words = grp[:].bitcast(F32).rearrange("p (c u) -> p c u", u=2)
-            tok_words = video_tok[g][:].bitcast(F32).rearrange("p (c k) -> p c k", c=COL_TILES)
-            transpose_and_group(tok_words, grp_words[:, EMBED:COLUMNS, :], False)
-            transpose_and_group(w_words[g], grp_words[:, 0:EMBED, :], g % 2 == 0)
+            transpose_and_group(video_tok[g], grp_words[:, EMBED:COLUMNS, :])
+            transpose_and_group(w_raw[g], grp_words[:, 0:EMBED, :])
             grouped[g] = grp
 
         def quantise(g):
@@ -136,31 +129,29 @@ def tile_tubeletembedding_k_kernel(tc, video, W, b, pos_embed, out):
             codes[g] = cod
             scales[g] = sca
 
-        def multiply(passes):
+        def multiply(g):
             for j in range(GRID):
                 tokens = slice(EMBED + j * P, EMBED + (j + 1) * P)
-                for g in passes:
-                    nc.tensor.matmul_mx(
-                        out=acc[j][:],
-                        lhsT=codes[g][:, tokens].bitcast(FP8X4),
-                        lhsT_scale=scales[g][:, tokens],
-                        rhs=codes[g][:, 0:EMBED].bitcast(FP8X4),
-                        rhs_scale=scales[g][:, 0:EMBED],
-                        start=(g == 0),
-                        stop=(g == PASSES - 1),
-                    )
+                nc.tensor.matmul_mx(
+                    out=acc[j][:],
+                    lhsT=codes[g][:, tokens].bitcast(FP8X4),
+                    lhsT_scale=scales[g][:, tokens],
+                    rhs=codes[g][:, 0:EMBED].bitcast(FP8X4),
+                    rhs_scale=scales[g][:, 0:EMBED],
+                    start=(g == 0),
+                    stop=(g == PASSES - 1),
+                )
 
         regroup(0)
-        regroup(1)
-        for s in range(PASSES + RUN):
-            if 1 <= s <= PASSES:
-                quantise(s - 1)
-            if s + 2 < PASSES:
-                regroup(s + 2)
+        for s in range(PASSES + MULTIPLY_LAG):
             if s < PASSES:
                 transpose(s)
-            if s % RUN == RUN - 1 and s >= 2 * RUN - 1:
-                multiply(range(s - 2 * RUN + 1, s - RUN + 1))
+            if 1 <= s <= PASSES:
+                quantise(s - 1)
+            if s >= MULTIPLY_LAG:
+                multiply(s - MULTIPLY_LAG)
+            if s + 1 < PASSES:
+                regroup(s + 1)
             j = s - (POS_AFTER_PASS + 2)
             if 0 <= j < GRID:
                 part = slice(j * EMBED, (j + 1) * EMBED)

from contextlib import ExitStack

import concourse.mybir as mybir
from concourse.masks import make_identity

BF16 = mybir.dt.bfloat16
F32 = mybir.dt.float32
U32 = mybir.dt.uint32
U8 = mybir.dt.uint8
FP8X4 = mybir.dt.float8_e4m3fn_x4

P = 128
BATCH, STACK, TUBE, IMG, PATCH, EMBED = 4, 16, 2, 256, 64, 512
GRID = IMG // PATCH
TUBES = STACK // TUBE
K = TUBE * PATCH * PATCH
K_PASS = 4 * P
PASSES = K // K_PASS
PASSES_PER_FRAME = PASSES // TUBE
ROWS_PER_PASS = K_PASS // PATCH
COL_TILES = 4
COLUMNS = 2 * EMBED

MULTIPLY_LAG = 2
POS_AFTER_PASS = 8

FLOPS = 2 * BATCH * TUBES * GRID * GRID * EMBED * K


def tile_tubeletembedding_k_kernel(tc, video, W, b, pos_embed, out):
    nc = tc.nc
    assert tuple(video.shape) == (BATCH, STACK, 1, IMG, IMG)
    assert tuple(W.shape) == (EMBED, K)
    assert BATCH * TUBES * GRID == P

    video_rows = video.rearrange("b (d t) c (i y) x -> t i (b d) (c y x)", t=TUBE, i=GRID)
    w_rows = W.rearrange("(c p) k -> p c k", p=P)
    pos_rows = pos_embed.rearrange("o (q j) e -> (o q) (j e)", j=GRID)
    out_rows = out.rearrange("b (q j) e -> (b q) j e", j=GRID)

    with ExitStack() as ctx:
        consts = ctx.enter_context(tc.tile_pool(name="consts", bufs=1))
        loaded = ctx.enter_context(tc.tile_pool(name="loaded", bufs=1))
        work = ctx.enter_context(tc.tile_pool(name="work", bufs=3))
        sums = ctx.enter_context(tc.psum_pool(name="sums", bufs=1))
        banks = ctx.enter_context(tc.psum_pool(name="banks", bufs=4))
        ctx.enter_context(tc.manual_schedule())

        video_raw = []
        w_raw = []
        pos_sb = consts.tile([P, GRID * EMBED], BF16)
        for g in range(PASSES):
            ts, y8 = divmod(g, PASSES_PER_FRAME)
            run = slice(y8 * ROWS_PER_PASS * IMG, (y8 + 1) * ROWS_PER_PASS * IMG)
            v_in = loaded.tile([P, ROWS_PER_PASS * IMG], BF16, name="v_in%d" % g)
            for i in range(GRID):
                nc.sync.dma_start(out=v_in[i:P:GRID, :], in_=video_rows[ts, i, :, run])
            w_in = loaded.tile([P, COL_TILES * K_PASS], BF16, name="w_in%d" % g)
            nc.sync.dma_start(
                out=w_in[:].rearrange("p (c k) -> p c k", c=COL_TILES),
                in_=w_rows[:, :, g * K_PASS : (g + 1) * K_PASS],
            )
            video_raw.append(v_in)
            w_raw.append(w_in)
            if g == POS_AFTER_PASS:
                for batch in range(BATCH):
                    rows = slice(batch * TUBES * GRID, (batch + 1) * TUBES * GRID)
                    nc.sync.dma_start(out=pos_sb[rows, :], in_=pos_rows)

        ident = consts.tile([P, P], F32)
        make_identity(nc, ident[:])

        bias_row = consts.tile([P, EMBED], BF16)
        nc.vector.memset(bias_row[:], 0.0)
        nc.scalar.dma_start(out=bias_row[0:1, :], in_=b.rearrange("(o e) -> o e", o=1))
        ones = consts.tile([P, P], BF16)
        nc.vector.memset(ones[:], 1.0)
        bias_bank = banks.tile([P, EMBED], F32, name="bank")
        nc.tensor.matmul(out=bias_bank[:], lhsT=ones[:], rhs=bias_row[:], start=True, stop=True)
        bias_all = consts.tile([P, EMBED], F32)
        nc.scalar.copy(out=bias_all[:], in_=bias_bank[:])

        addend = consts.tile([P, GRID * EMBED], F32)
        result = consts.tile([P, GRID * EMBED], F32)
        acc = []
        for j in range(GRID):
            acc_j = sums.tile([P, EMBED], F32, name="acc%d" % j)
            acc.append(acc_j)

        video_tok = {}
        grouped = {}
        codes = {}
        scales = {}

        def regroup(g):
            v_tok = work.tile([P, COL_TILES * K_PASS], BF16, name="v_tok")
            nc.vector.tensor_copy(
                out=v_tok[:].bitcast(F32).rearrange("p (j y w) -> p j y w", j=GRID, w=PATCH // 2),
                in_=video_raw[g][:].bitcast(F32).rearrange("p (y j w) -> p j y w", j=GRID, w=PATCH // 2),
            )
            video_tok[g] = v_tok

        def transpose_and_group(source, target_words):
            words = source[:].bitcast(F32)
            for pair in range(COL_TILES // 2):
                bank = banks.tile([P, 2, 2 * P], F32, name="bank")
                for c in range(2):
                    for u in range(2):
                        first = ((2 * pair + c) * 2 + u) * P
                        nc.tensor.transpose(
                            bank[:, u, c * P : (c + 1) * P], words[:, first : first + P], ident[:]
                        )
                nc.scalar.copy(
                    out=target_words[:, pair * 2 * P : (pair + 1) * 2 * P, :],
                    in_=bank[:].rearrange("p u c -> p c u"),
                )

        def transpose(g):
            grp = work.tile([P, COLUMNS * 4], BF16, name="grp", align_bytes=64)
            grp_words = grp[:].bitcast(F32).rearrange("p (c u) -> p c u", u=2)
            transpose_and_group(video_tok[g], grp_words[:, EMBED:COLUMNS, :])
            transpose_and_group(w_raw[g], grp_words[:, 0:EMBED, :])
            grouped[g] = grp

        def quantise(g):
            cod = work.tile([P, COLUMNS], U32, name="cod", align_bytes=64)
            sca = work.tile([P, COLUMNS], U8, name="sca", align_bytes=64)
            nc.vector.quantize_mx(out=cod[:].bitcast(FP8X4), scales=sca[:], in_=grouped[g][:])
            codes[g] = cod
            scales[g] = sca

        def multiply(g):
            for j in range(GRID):
                tokens = slice(EMBED + j * P, EMBED + (j + 1) * P)
                nc.tensor.matmul_mx(
                    out=acc[j][:],
                    lhsT=codes[g][:, tokens].bitcast(FP8X4),
                    lhsT_scale=scales[g][:, tokens],
                    rhs=codes[g][:, 0:EMBED].bitcast(FP8X4),
                    rhs_scale=scales[g][:, 0:EMBED],
                    start=(g == 0),
                    stop=(g == PASSES - 1),
                )

        regroup(0)
        for s in range(PASSES + MULTIPLY_LAG):
            if s < PASSES:
                transpose(s)
            if 1 <= s <= PASSES:
                quantise(s - 1)
            if s >= MULTIPLY_LAG:
                multiply(s - MULTIPLY_LAG)
            if s + 1 < PASSES:
                regroup(s + 1)
            j = s - (POS_AFTER_PASS + 2)
            if 0 <= j < GRID:
                part = slice(j * EMBED, (j + 1) * EMBED)
                nc.vector.tensor_tensor(
                    out=addend[:, part], in0=pos_sb[:, part], in1=bias_all[:], op=mybir.AluOpType.add
                )

        for j in range(GRID):
            part = slice(j * EMBED, (j + 1) * EMBED)
            nc.vector.tensor_tensor(
                out=result[:, part], in0=acc[j][:], in1=addend[:, part], op=mybir.AluOpType.add
            )
            nc.sync.dma_start(out=out_rows[:, j, :], in_=result[:, part])
